import numpy as np
import ml_dtypes


def mxq(x, axis, fmt="e4m3"):
    dtype, down = {"e4m3": (ml_dtypes.float8_e4m3fn, 7), "e5m2": (ml_dtypes.float8_e5m2, 14)}[fmt]
    v = np.moveaxis(np.asarray(x, np.float32).astype(ml_dtypes.bfloat16).astype(np.float64), axis, -1)
    blocks = v.reshape(v.shape[:-1] + (-1, 32))
    amax = np.abs(blocks).max(-1, keepdims=True)
    byte = np.maximum(np.where(amax > 0, np.frexp(amax)[1] - 1 + 127, 0) - down, 1)
    scale = np.exp2(byte - 127.0)
    codes = (blocks / scale).astype(np.float32).astype(dtype).astype(np.float64)
    return np.moveaxis((codes * scale).reshape(v.shape), -1, axis)


WIDE = False


def mx_kscale(k):
    if not WIDE:
        return np.ones(k)
    levels = np.array([10, -10, 5, -5, 0])
    if k % 512:
        return np.exp2(np.random.permutation(np.resize(levels, k // 32))).repeat(32)
    a = np.empty((k // 512, 16))
    for p in range(k // 512):
        a[p, :8] = np.random.permutation(np.resize(levels, 8))
        for g in range(8):
            far = levels[np.abs(levels - a[p, g]) >= 10]
            a[p, g + 8] = far[np.random.randint(len(far))]
    return np.exp2(a.ravel()).repeat(32)


BF16 = ml_dtypes.bfloat16


def bf(x):
    return np.asarray(x, np.float32).astype(BF16)


def f64(x):
    return np.asarray(x).astype(np.float64)


B, S, H, I, G = 1, 128, 512, 512, 4
T = B * S


def grouped_linear(xf, w, b):
    g, dout, din = w.shape
    xg = xf.reshape(g, -1, din)
    y = (mxq(xg, 2, "e4m3") @ mxq(w, 2, "e4m3").transpose(0, 2, 1)) + b[:, None, :]
    return y.reshape(-1, dout)


def setup_inputs():
    s, t = mx_kscale(H), mx_kscale(I)
    return {"hf": bf(np.random.standard_normal((T, H)) * s),
            "g1_w": bf(np.random.standard_normal((G, I, H)) / np.sqrt(H) / s[None, None, :] * t[None, :, None]),
            "g1_b": bf(np.random.standard_normal((G, I)) * 0.3 * t[None, :]),
            "g2_w": bf(np.random.standard_normal((G, H, I)) / np.sqrt(I) / t[None, None, :]),
            "g2_b": bf(np.random.standard_normal((G, H)) * 0.3)}


def reference(hf, g1_w, g1_b, g2_w, g2_b):
    y = grouped_linear(f64(hf), f64(g1_w), f64(g1_b))
    return grouped_linear(y, f64(g2_w), f64(g2_b))

@@ -1,0 +1,189 @@
+from contextlib import ExitStack
+
+import concourse.mybir as mybir
+from concourse.masks import make_identity
+
+BF16 = mybir.dt.bfloat16
+F32 = mybir.dt.float32
+I32 = mybir.dt.int32
+U32 = mybir.dt.uint32
+U8 = mybir.dt.uint8
+FP8X4 = mybir.dt.float8_e4m3fn_x4
+
+P = 128
+PACK = 4
+K = P * PACK
+HALVES = 2
+GROUPS = 4
+TOKENS = 128
+GROUP_TOKENS = TOKENS // GROUPS
+FEATURES = 512
+BLOCKS = FEATURES // P
+BLOCKS_PER_BANK = 2
+LAG = 2
+WARM_PASSES = 6
+
+FLOPS = 2 * 2 * TOKENS * K * FEATURES
+
+
+def k_to_partitions(nc, banks, stage, identity, rows, blocks, tag):
+    words = rows.bitcast(F32)
+    grouped = stage.tile([P, blocks * P * PACK], BF16, align_bytes=64, tag=tag, name=tag)
+    grouped_words = grouped[:].bitcast(F32).rearrange("p (b r u) -> p b r u", r=P, u=HALVES)
+    for first in range(0, blocks, BLOCKS_PER_BANK):
+        count = min(BLOCKS_PER_BANK, blocks - first)
+        bank = banks.tile([P, count, HALVES, P], F32, tag="bank", name="bank")
+        for b in range(count):
+            for u in range(HALVES):
+                start = (first + b) * HALVES * P
+                every_second = slice(start + u, start + HALVES * P, HALVES)
+                nc.tensor.transpose(bank[:, b, u, :], words[:, every_second], identity)
+        nc.scalar.copy(
+            out=grouped_words[:, first : first + count],
+            in_=bank[:].rearrange("p b u r -> p b r u"),
+        )
+    return grouped
+
+
+def quantise(nc, keep, grouped, name):
+    columns = grouped.shape[1] // PACK
+    codes = keep.tile([P, columns], U32, align_bytes=64, name=name + "_codes")
+    scales = keep.tile([P, columns], U8, align_bytes=64, name=name + "_scales")
+    nc.vector.quantize_mx(out=codes[:].bitcast(FP8X4), scales=scales[:], in_=grouped[:])
+    return codes, scales
+
+
+def tile_dummytemodel_pa_s_kernel(tc, hf, g1_w, g1_b, g2_w, g2_b, out):
+    nc = tc.nc
+    with ExitStack() as ctx:
+        ctx.enter_context(tc.manual_schedule())
+        keep = ctx.enter_context(tc.tile_pool(name="keep", bufs=1))
+        stage = ctx.enter_context(tc.tile_pool(name="stage", bufs=3))
+        banks = ctx.enter_context(tc.psum_pool(name="banks", bufs=7))
+        out_bank = ctx.enter_context(tc.psum_pool(name="out_bank", bufs=1))
+
+        hf_rows = keep.tile([P, K], BF16)
+        nc.sync.dma_start(out=hf_rows[:], in_=hf)
+        b1_rows = keep.tile([P, K], BF16)
+        nc.vector.memset(b1_rows[:].bitcast(I32), 0)
+        nc.sync.dma_start(out=b1_rows[0:GROUPS, :], in_=g1_b)
+        w1_rows = []
+        w2_rows = []
+        for g in range(GROUPS):
+            rows = keep.tile([P, BLOCKS * K], BF16, name="w1_rows%d" % g)
+            nc.sync.dma_start(out=rows[:], in_=g1_w[g].rearrange("(r t) k -> r (t k)", t=BLOCKS))
+            w1_rows.append(rows)
+        for g in range(GROUPS):
+            rows = keep.tile([P, BLOCKS * K], BF16, name="w2_rows%d" % g)
+            nc.sync.dma_start(out=rows[:], in_=g2_w[g].rearrange("(r j) k -> r (j k)", j=BLOCKS))
+            w2_rows.append(rows)
+        b2_rows = keep.tile([P, FEATURES], BF16)
+        for g in range(GROUPS):
+            nc.sync.dma_start(
+                out=b2_rows[g * GROUP_TOKENS : (g + 1) * GROUP_TOKENS, :],
+                in_=g2_b[g].partition_broadcast(GROUP_TOKENS),
+            )
+
+        identity = keep.tile([P, P], F32)
+        make_identity(nc, identity[:])
+
+        y_grouped = keep.tile([P, GROUPS, TOKENS, PACK], BF16, align_bytes=64)
+        y_codes = keep.tile([P, GROUPS, TOKENS], U32, align_bytes=64)
+        y_scales = keep.tile([P, GROUPS, TOKENS], U8, align_bytes=64)
+        nc.vector.memset(y_grouped[:].rearrange("p g t c -> p (g t c)").bitcast(I32), 0)
+        nc.vector.quantize_mx(
+            out=y_codes[:].rearrange("p g t -> p (g t)").bitcast(FP8X4),
+            scales=y_scales[:].rearrange("p g t -> p (g t)"),
+            in_=y_grouped[:].rearrange("p g t c -> p (g t c)"),
+        )
+
+        def keep_warm(passes):
+            unread = banks.tile([P, FEATURES], F32, tag="bank", name="bank")
+            for n in range(passes):
+                nc.tensor.matmul_mx(
+                    out=unread[:],
+                    lhsT=y_codes[:, 0, :].bitcast(FP8X4),
+                    lhsT_scale=y_scales[:, 0, :],
+                    rhs=y_codes[:].rearrange("p g t -> p (g t)").bitcast(FP8X4),
+                    rhs_scale=y_scales[:].rearrange("p g t -> p (g t)"),
+                    start=True,
+                    stop=True,
+                )
+
+        keep_warm(WARM_PASSES)
+
+        x_grouped = k_to_partitions(nc, banks, stage, identity[:], hf_rows[:], 1, "x_grouped")
+        x_codes, x_scales = quantise(nc, keep, x_grouped, "x")
+
+        b1_bank = banks.tile([P, HALVES, P], F32, tag="bank", name="bank")
+        for u in range(HALVES):
+            nc.tensor.transpose(b1_bank[:, u, :], b1_rows[:].bitcast(F32)[:, u::HALVES], identity[:])
+        b1_cols = keep.tile([P, GROUPS * PACK], F32)
+        for u in range(HALVES):
+            nc.vector.tensor_copy(
+                out=b1_cols[:].rearrange("p (g u e) -> p u g e", g=GROUPS, u=HALVES)[:, u],
+                in_=b1_bank[:, u, 0:GROUPS].bitcast(BF16).rearrange("p (g e) -> p g e", e=2),
+            )
+
+        acc = out_bank.tile([P, FEATURES], F32)
+
+        def layer_1(g, codes, scales):
+            y_bank = banks.tile([P, PACK, TOKENS], F32, tag="bank", name="bank")
+            for t in range(PACK):
+                block = slice(t * P, (t + 1) * P)
+                nc.tensor.matmul_mx(
+                    out=y_bank[:, t, :],
+                    lhsT=codes[:, block].bitcast(FP8X4),
+                    lhsT_scale=scales[:, block],
+                    rhs=x_codes[:].bitcast(FP8X4),
+                    rhs_scale=x_scales[:],
+                    start=True,
+                    stop=True,
+                )
+            own = slice(g * GROUP_TOKENS, (g + 1) * GROUP_TOKENS)
+            nc.vector.tensor_tensor(
+                out=y_grouped[:, g, own, :],
+                in0=y_bank[:, :, own].rearrange("p c t -> p t c"),
+                in1=b1_cols[:, g * PACK : (g + 1) * PACK]
+                .unsqueeze(1)
+                .to_broadcast([P, GROUP_TOKENS, PACK]),
+                op=mybir.AluOpType.add,
+            )
+            nc.vector.quantize_mx(
+                out=y_codes[:, g, :].bitcast(FP8X4),
+                scales=y_scales[:, g, :],
+                in_=y_grouped[:, g].rearrange("p t c -> p (t c)"),
+            )
+
+        def layer_2(g, codes, scales):
+            nc.tensor.matmul_mx(
+                out=acc[:],
+                lhsT=y_codes[:, g, :].bitcast(FP8X4),
+                lhsT_scale=y_scales[:, g, :],
+                rhs=codes[:].bitcast(FP8X4),
+                rhs_scale=scales[:],
+                start=(g == 0),
+                stop=(g == GROUPS - 1),
+            )
+
+        w_rows = w1_rows + w2_rows
+        w_quantised = []
+        for i in range(len(w_rows) + LAG):
+            if i < len(w_rows):
+                grouped = k_to_partitions(nc, banks, stage, identity[:], w_rows[i][:], BLOCKS, "w_grouped")
+                w_quantised.append(quantise(nc, keep, grouped, "w%d" % i))
+            if i < LAG:
+                keep_warm(1)
+            elif i < LAG + GROUPS:
+                layer_1(i - LAG, *w_quantised[i - LAG])
+            else:
+                layer_2(i - LAG - GROUPS, *w_quantised[i - LAG])
+
+        result = keep.tile([P, FEATURES], F32)
+        nc.vector.tensor_tensor(
+            out=result[:].rearrange("p (r j) -> p r j", j=BLOCKS),
+            in0=acc[:].rearrange("p (j r) -> p r j", j=BLOCKS),
+            in1=b2_rows[:].rearrange("p (r j) -> p r j", j=BLOCKS),
+            op=mybir.AluOpType.add,
+        )
+        nc.sync.dma_start(out=out, in_=result[:])

@@ -9,6 +9,7 @@ I32 = mybir.dt.int32
 U32 = mybir.dt.uint32
 U8 = mybir.dt.uint8
 FP8X4 = mybir.dt.float8_e4m3fn_x4
+ADD = mybir.AluOpType.add
 
 P = 128
 PACK = 4
@@ -18,39 +19,11 @@ GROUPS = 4
 TOKENS = 128
 GROUP_TOKENS = TOKENS // GROUPS
 FEATURES = 512
-BLOCKS = FEATURES // P
-BLOCKS_PER_BANK = 2
-LAG = 2
-WARM_PASSES = 6
+PAIR = 2
+UNITS = FEATURES // P // PAIR
+UNIT_FEATURES = PAIR * P
 
 FLOPS = 2 * 2 * TOKENS * K * FEATURES
-
-
-def k_to_partitions(nc, banks, stage, identity, rows, blocks, tag):
-    words = rows.bitcast(F32)
-    grouped = stage.tile([P, blocks * P * PACK], BF16, align_bytes=64, tag=tag, name=tag)
-    grouped_words = grouped[:].bitcast(F32).rearrange("p (b r u) -> p b r u", r=P, u=HALVES)
-    for first in range(0, blocks, BLOCKS_PER_BANK):
-        count = min(BLOCKS_PER_BANK, blocks - first)
-        bank = banks.tile([P, count, HALVES, P], F32, tag="bank", name="bank")
-        for b in range(count):
-            for u in range(HALVES):
-                start = (first + b) * HALVES * P
-                every_second = slice(start + u, start + HALVES * P, HALVES)
-                nc.tensor.transpose(bank[:, b, u, :], words[:, every_second], identity)
-        nc.scalar.copy(
-            out=grouped_words[:, first : first + count],
-            in_=bank[:].rearrange("p b u r -> p b r u"),
-        )
-    return grouped
-
-
-def quantise(nc, keep, grouped, name):
-    columns = grouped.shape[1] // PACK
-    codes = keep.tile([P, columns], U32, align_bytes=64, name=name + "_codes")
-    scales = keep.tile([P, columns], U8, align_bytes=64, name=name + "_scales")
-    nc.vector.quantize_mx(out=codes[:].bitcast(FP8X4), scales=scales[:], in_=grouped[:])
-    return codes, scales
 
 
 def tile_dummytemodel_pa_s_kernel(tc, hf, g1_w, g1_b, g2_w, g2_b, out):
@@ -58,31 +31,43 @@ def tile_dummytemodel_pa_s_kernel(tc, hf, g1_w, g1_b, g2_w, g2_b, out):
     with ExitStack() as ctx:
         ctx.enter_context(tc.manual_schedule())
         keep = ctx.enter_context(tc.tile_pool(name="keep", bufs=1))
-        stage = ctx.enter_context(tc.tile_pool(name="stage", bufs=3))
-        banks = ctx.enter_context(tc.psum_pool(name="banks", bufs=7))
-        out_bank = ctx.enter_context(tc.psum_pool(name="out_bank", bufs=1))
+        stage = ctx.enter_context(tc.tile_pool(name="stage", bufs=4))
+        banks = ctx.enter_context(tc.psum_pool(name="banks", bufs=4))
+        y_banks = ctx.enter_context(tc.psum_pool(name="y_banks", bufs=2))
+        sums = ctx.enter_context(tc.psum_pool(name="sums", bufs=1))
 
         hf_rows = keep.tile([P, K], BF16)
         nc.sync.dma_start(out=hf_rows[:], in_=hf)
         b1_rows = keep.tile([P, K], BF16)
         nc.vector.memset(b1_rows[:].bitcast(I32), 0)
-        nc.sync.dma_start(out=b1_rows[0:GROUPS, :], in_=g1_b)
-        w1_rows = []
-        w2_rows = []
-        for g in range(GROUPS):
-            rows = keep.tile([P, BLOCKS * K], BF16, name="w1_rows%d" % g)
-            nc.sync.dma_start(out=rows[:], in_=g1_w[g].rearrange("(r t) k -> r (t k)", t=BLOCKS))
-            w1_rows.append(rows)
-        for g in range(GROUPS):
-            rows = keep.tile([P, BLOCKS * K], BF16, name="w2_rows%d" % g)
-            nc.sync.dma_start(out=rows[:], in_=g2_w[g].rearrange("(r j) k -> r (j k)", j=BLOCKS))
-            w2_rows.append(rows)
         b2_rows = keep.tile([P, FEATURES], BF16)
+
+        rows = []
+
+        def load(i, whole):
+            if i < GROUPS:
+                view = g1_w[i].rearrange("(r c j) k -> r c (j k)", c=UNITS, j=PAIR)
+            else:
+                view = g2_w[i - GROUPS].rearrange("(c r j) k -> r c (j k)", c=UNITS, j=PAIR)
+            tile = keep.tile([P, UNITS, PAIR * K], BF16, name="w_rows%d" % i)
+            if whole:
+                nc.sync.dma_start(out=tile[:], in_=view)
+            else:
+                for c in range(UNITS):
+                    nc.sync.dma_start(out=tile[:, c, :], in_=view[:, c, :])
+            rows.append(tile)
+
+        load(0, False)
+        nc.sync.dma_start(out=b1_rows[0:GROUPS, :], in_=g1_b)
+        for i in range(1, 6):
+            load(i, True)
         for g in range(GROUPS):
             nc.sync.dma_start(
                 out=b2_rows[g * GROUP_TOKENS : (g + 1) * GROUP_TOKENS, :],
                 in_=g2_b[g].partition_broadcast(GROUP_TOKENS),
             )
+        load(6, True)
+        load(7, False)
 
         identity = keep.tile([P, P], F32)
         make_identity(nc, identity[:])
@@ -91,50 +76,77 @@ def tile_dummytemodel_pa_s_kernel(tc, hf, g1_w, g1_b, g2_w, g2_b, out):
         y_codes = keep.tile([P, GROUPS, TOKENS], U32, align_bytes=64)
         y_scales = keep.tile([P, GROUPS, TOKENS], U8, align_bytes=64)
         nc.vector.memset(y_grouped[:].rearrange("p g t c -> p (g t c)").bitcast(I32), 0)
-        nc.vector.quantize_mx(
-            out=y_codes[:].rearrange("p g t -> p (g t)").bitcast(FP8X4),
-            scales=y_scales[:].rearrange("p g t -> p (g t)"),
-            in_=y_grouped[:].rearrange("p g t c -> p (g t c)"),
-        )
 
-        def keep_warm(passes):
-            unread = banks.tile([P, FEATURES], F32, tag="bank", name="bank")
-            for n in range(passes):
-                nc.tensor.matmul_mx(
-                    out=unread[:],
-                    lhsT=y_codes[:, 0, :].bitcast(FP8X4),
-                    lhsT_scale=y_scales[:, 0, :],
-                    rhs=y_codes[:].rearrange("p g t -> p (g t)").bitcast(FP8X4),
-                    rhs_scale=y_scales[:].rearrange("p g t -> p (g t)"),
-                    start=True,
-                    stop=True,
+        def transposes(words, bank, first, count):
+            for b in range(count):
+                start = (first + b) * HALVES * P
+                for u in range(HALVES):
+                    nc.tensor.transpose(
+                        bank[:, b, u, :], words[:, start + u : start + HALVES * P : HALVES], identity[:]
+                    )
+
+        def copy_out(engine, bank, grouped, first, count):
+            out_words = grouped[:].bitcast(F32).rearrange("p (b r u) -> p b r u", r=P, u=HALVES)
+            out_words = out_words[:, first : first + count]
+            in_words = bank[:].rearrange("p b u r -> p b r u")
+            if engine == "S":
+                nc.scalar.copy(out=out_words, in_=in_words)
+            else:
+                nc.vector.tensor_copy(out=out_words, in_=in_words)
+
+        x_bank = banks.tile([P, 1, HALVES, P], F32, tag="bank", name="x_bank")
+        transposes(hf_rows[:].bitcast(F32), x_bank, 0, 1)
+        x_grouped = stage.tile([P, P * PACK], BF16, align_bytes=64, tag="x", name="x_grouped")
+        copy_out("S", x_bank, x_grouped, 0, 1)
+        x_codes = keep.tile([P, P], U32, align_bytes=64)
+        x_scales = keep.tile([P, P], U8, align_bytes=64)
+        nc.vector.quantize_mx(out=x_codes[:].bitcast(FP8X4), scales=x_scales[:], in_=x_grouped[:])
+
+        codes = {}
+        pending = []
+
+        def turn(i, c, engine):
+            words = rows[i][:, c, :].bitcast(F32)
+            grouped = stage.tile([P, PAIR * P * PACK], BF16, align_bytes=64, tag="w", name="w_grouped")
+            if engine == "VS":
+                for b, e in enumerate("VS"):
+                    bank = banks.tile([P, 1, HALVES, P], F32, tag="bank", name="bank")
+                    transposes(words, bank, b, 1)
+                    copy_out(e, bank, grouped, b, 1)
+            else:
+                bank = banks.tile([P, PAIR, HALVES, P], F32, tag="bank", name="bank")
+                transposes(words, bank, 0, PAIR)
+                copy_out(engine, bank, grouped, 0, PAIR)
+            pending.append((i, c, grouped))
+
+        def quantise():
+            i, c, grouped = pending.pop(0)
+            q = keep.tile([P, UNIT_FEATURES], U32, align_bytes=64, name="codes%d_%d" % (i, c))
+            s = keep.tile([P, UNIT_FEATURES], U8, align_bytes=64, name="scales%d_%d" % (i, c))
+            nc.vector.quantize_mx(out=q[:].bitcast(FP8X4), scales=s[:], in_=grouped[:])
+            codes[i, c] = (q, s)
+
+        b1_cols = keep.tile([P, GROUPS * PACK], F32)
+
+        def bias_1():
+            b1_bank = banks.tile([P, HALVES, P], F32, tag="bank", name="b1_bank")
+            for u in range(HALVES):
+                nc.tensor.transpose(b1_bank[:, u, :], b1_rows[:].bitcast(F32)[:, u::HALVES], identity[:])
+            for u in range(HALVES):
+                nc.vector.tensor_copy(
+                    out=b1_cols[:].rearrange("p (g u e) -> p u g e", g=GROUPS, u=HALVES)[:, u],
+                    in_=b1_bank[:, u, 0:GROUPS].bitcast(BF16).rearrange("p (g e) -> p g e", e=2),
                 )
 
-        keep_warm(WARM_PASSES)
-
-        x_grouped = k_to_partitions(nc, banks, stage, identity[:], hf_rows[:], 1, "x_grouped")
-        x_codes, x_scales = quantise(nc, keep, x_grouped, "x")
-
-        b1_bank = banks.tile([P, HALVES, P], F32, tag="bank", name="bank")
-        for u in range(HALVES):
-            nc.tensor.transpose(b1_bank[:, u, :], b1_rows[:].bitcast(F32)[:, u::HALVES], identity[:])
-        b1_cols = keep.tile([P, GROUPS * PACK], F32)
-        for u in range(HALVES):
-            nc.vector.tensor_copy(
-                out=b1_cols[:].rearrange("p (g u e) -> p u g e", g=GROUPS, u=HALVES)[:, u],
-                in_=b1_bank[:, u, 0:GROUPS].bitcast(BF16).rearrange("p (g e) -> p g e", e=2),
-            )
-
-        acc = out_bank.tile([P, FEATURES], F32)
-
-        def layer_1(g, codes, scales):
-            y_bank = banks.tile([P, PACK, TOKENS], F32, tag="bank", name="bank")
+        def layer_1(g):
+            y_bank = y_banks.tile([P, PACK, TOKENS], F32, tag="y_bank", name="y_bank")
             for t in range(PACK):
-                block = slice(t * P, (t + 1) * P)
+                q, s = codes[g, t // PAIR]
+                block = slice((t % PAIR) * P, (t % PAIR + 1) * P)
                 nc.tensor.matmul_mx(
                     out=y_bank[:, t, :],
-                    lhsT=codes[:, block].bitcast(FP8X4),
-                    lhsT_scale=scales[:, block],
+                    lhsT=q[:, block].bitcast(FP8X4),
+                    lhsT_scale=s[:, block],
                     rhs=x_codes[:].bitcast(FP8X4),
                     rhs_scale=x_scales[:],
                     start=True,
@@ -144,46 +156,84 @@ def tile_dummytemodel_pa_s_kernel(tc, hf, g1_w, g1_b, g2_w, g2_b, out):
             nc.vector.tensor_tensor(
                 out=y_grouped[:, g, own, :],
                 in0=y_bank[:, :, own].rearrange("p c t -> p t c"),
-                in1=b1_cols[:, g * PACK : (g + 1) * PACK]
-                .unsqueeze(1)
-                .to_broadcast([P, GROUP_TOKENS, PACK]),
-                op=mybir.AluOpType.add,
+                in1=b1_cols[:, g * PACK : (g + 1) * PACK].unsqueeze(1).to_broadcast([P, GROUP_TOKENS, PACK]),
+                op=ADD,
             )
+
+        def quantise_y(g):
             nc.vector.quantize_mx(
                 out=y_codes[:, g, :].bitcast(FP8X4),
                 scales=y_scales[:, g, :],
                 in_=y_grouped[:, g].rearrange("p t c -> p (t c)"),
             )
 
-        def layer_2(g, codes, scales):
+        acc = [sums.tile([P, UNIT_FEATURES], F32, name="acc%d" % c) for c in range(UNITS)]
+
+        def layer_2(g, c):
+            q, s = codes[GROUPS + g, c]
             nc.tensor.matmul_mx(
-                out=acc[:],
+                out=acc[c][:],
                 lhsT=y_codes[:, g, :].bitcast(FP8X4),
                 lhsT_scale=y_scales[:, g, :],
-                rhs=codes[:].bitcast(FP8X4),
-                rhs_scale=scales[:],
+                rhs=q[:].bitcast(FP8X4),
+                rhs_scale=s[:],
                 start=(g == 0),
                 stop=(g == GROUPS - 1),
             )
 
-        w_rows = w1_rows + w2_rows
-        w_quantised = []
-        for i in range(len(w_rows) + LAG):
-            if i < len(w_rows):
-                grouped = k_to_partitions(nc, banks, stage, identity[:], w_rows[i][:], BLOCKS, "w_grouped")
-                w_quantised.append(quantise(nc, keep, grouped, "w%d" % i))
-            if i < LAG:
-                keep_warm(1)
-            elif i < LAG + GROUPS:
-                layer_1(i - LAG, *w_quantised[i - LAG])
-            else:
-                layer_2(i - LAG - GROUPS, *w_quantised[i - LAG])
-
+        turn(0, 0, "S")
+        turn(0, 1, "S")
+        quantise()
+        bias_1()
+        turn(1, 0, "S")
+        quantise()
+        turn(1, 1, "V")
+        quantise()
+        turn(2, 0, "S")
+        quantise()
+        turn(2, 1, "S")
+        quantise()
+        layer_1(0)
+        layer_1(1)
+        turn(3, 0, "S")
+        quantise()
+        quantise_y(0)
+        quantise_y(1)
+        turn(3, 1, "V")
+        quantise()
+        turn(4, 0, "S")
+        quantise()
+        turn(4, 1, "S")
+        quantise()
+        layer_1(2)
+        layer_1(3)
+        turn(5, 0, "S")
+        quantise()
+        quantise_y(2)
+        quantise_y(3)
+        turn(5, 1, "V")
+        quantise()
+        turn(6, 0, "S")
+        quantise()
+        turn(6, 1, "S")
+        quantise()
+        turn(7, 0, "S")
+        quantise()
+        turn(7, 1, "VS")
+        quantise()
+        quantise()
+        for c in range(UNITS):
+            for g in range(GROUPS - 1):
+                layer_2(g, c)
         result = keep.tile([P, FEATURES], F32)
-        nc.vector.tensor_tensor(
-            out=result[:].rearrange("p (r j) -> p r j", j=BLOCKS),
-            in0=acc[:].rearrange("p (j r) -> p r j", j=BLOCKS),
-            in1=b2_rows[:].rearrange("p (r j) -> p r j", j=BLOCKS),
-            op=mybir.AluOpType.add,
-        )
-        nc.sync.dma_start(out=out, in_=result[:])
+        for c in range(UNITS):
+            layer_2(GROUPS - 1, c)
+        for c in range(UNITS):
+            cols = slice(c * UNIT_FEATURES, (c + 1) * UNIT_FEATURES)
+            nc.vector.tensor_tensor(
+                out=result[:, cols].rearrange("p (r j) -> p r j", j=PAIR),
+                in0=acc[c][:].rearrange("p (j r) -> p r j", j=PAIR),
+                in1=b2_rows[:, cols].rearrange("p (r j) -> p r j", j=PAIR),
+                op=ADD,
+            )
+            nc.sync.dma_start(out=out[:, cols], in_=result[:, cols])

@@ -59,15 +59,14 @@ def tile_dummytemodel_pa_s_kernel(tc, hf, g1_w, g1_b, g2_w, g2_b, out):
 
         load(0, False)
         nc.sync.dma_start(out=b1_rows[0:GROUPS, :], in_=g1_b)
-        for i in range(1, 6):
+        for i in range(1, 7):
             load(i, True)
+        load(7, False)
         for g in range(GROUPS):
             nc.sync.dma_start(
                 out=b2_rows[g * GROUP_TOKENS : (g + 1) * GROUP_TOKENS, :],
                 in_=g2_b[g].partition_broadcast(GROUP_TOKENS),
             )
-        load(6, True)
-        load(7, False)
 
         identity = keep.tile([P, P], F32)
         make_identity(nc, identity[:])

from contextlib import ExitStack

import concourse.mybir as mybir
from concourse.masks import make_identity

BF16 = mybir.dt.bfloat16
F32 = mybir.dt.float32
I32 = mybir.dt.int32
U32 = mybir.dt.uint32
U8 = mybir.dt.uint8
FP8X4 = mybir.dt.float8_e4m3fn_x4
ADD = mybir.AluOpType.add

P = 128
PACK = 4
K = P * PACK
HALVES = 2
GROUPS = 4
TOKENS = 128
GROUP_TOKENS = TOKENS // GROUPS
FEATURES = 512
PAIR = 2
UNITS = FEATURES // P // PAIR
UNIT_FEATURES = PAIR * P

FLOPS = 2 * 2 * TOKENS * K * FEATURES


def tile_dummytemodel_pa_s_kernel(tc, hf, g1_w, g1_b, g2_w, g2_b, out):
    nc = tc.nc
    with ExitStack() as ctx:
        ctx.enter_context(tc.manual_schedule())
        keep = ctx.enter_context(tc.tile_pool(name="keep", bufs=1))
        stage = ctx.enter_context(tc.tile_pool(name="stage", bufs=4))
        banks = ctx.enter_context(tc.psum_pool(name="banks", bufs=4))
        y_banks = ctx.enter_context(tc.psum_pool(name="y_banks", bufs=2))
        sums = ctx.enter_context(tc.psum_pool(name="sums", bufs=1))

        hf_rows = keep.tile([P, K], BF16)
        nc.sync.dma_start(out=hf_rows[:], in_=hf)
        b1_rows = keep.tile([P, K], BF16)
        nc.vector.memset(b1_rows[:].bitcast(I32), 0)
        b2_rows = keep.tile([P, FEATURES], BF16)

        rows = []

        def load(i, whole):
            if i < GROUPS:
                view = g1_w[i].rearrange("(r c j) k -> r c (j k)", c=UNITS, j=PAIR)
            else:
                view = g2_w[i - GROUPS].rearrange("(c r j) k -> r c (j k)", c=UNITS, j=PAIR)
            tile = keep.tile([P, UNITS, PAIR * K], BF16, name="w_rows%d" % i)
            if whole:
                nc.sync.dma_start(out=tile[:], in_=view)
            else:
                for c in range(UNITS):
                    nc.sync.dma_start(out=tile[:, c, :], in_=view[:, c, :])
            rows.append(tile)

        load(0, False)
        nc.sync.dma_start(out=b1_rows[0:GROUPS, :], in_=g1_b)
        for i in range(1, 7):
            load(i, True)
        load(7, False)
        for g in range(GROUPS):
            nc.sync.dma_start(
                out=b2_rows[g * GROUP_TOKENS : (g + 1) * GROUP_TOKENS, :],
                in_=g2_b[g].partition_broadcast(GROUP_TOKENS),
            )

        identity = keep.tile([P, P], F32)
        make_identity(nc, identity[:])

        y_grouped = keep.tile([P, GROUPS, TOKENS, PACK], BF16, align_bytes=64)
        y_codes = keep.tile([P, GROUPS, TOKENS], U32, align_bytes=64)
        y_scales = keep.tile([P, GROUPS, TOKENS], U8, align_bytes=64)
        nc.vector.memset(y_grouped[:].rearrange("p g t c -> p (g t c)").bitcast(I32), 0)

        def transposes(words, bank, first, count):
            for b in range(count):
                start = (first + b) * HALVES * P
                for u in range(HALVES):
                    nc.tensor.transpose(
                        bank[:, b, u, :], words[:, start + u : start + HALVES * P : HALVES], identity[:]
                    )

        def copy_out(engine, bank, grouped, first, count):
            out_words = grouped[:].bitcast(F32).rearrange("p (b r u) -> p b r u", r=P, u=HALVES)
            out_words = out_words[:, first : first + count]
            in_words = bank[:].rearrange("p b u r -> p b r u")
            if engine == "S":
                nc.scalar.copy(out=out_words, in_=in_words)
            else:
                nc.vector.tensor_copy(out=out_words, in_=in_words)

        x_bank = banks.tile([P, 1, HALVES, P], F32, tag="bank", name="x_bank")
        transposes(hf_rows[:].bitcast(F32), x_bank, 0, 1)
        x_grouped = stage.tile([P, P * PACK], BF16, align_bytes=64, tag="x", name="x_grouped")
        copy_out("S", x_bank, x_grouped, 0, 1)
        x_codes = keep.tile([P, P], U32, align_bytes=64)
        x_scales = keep.tile([P, P], U8, align_bytes=64)
        nc.vector.quantize_mx(out=x_codes[:].bitcast(FP8X4), scales=x_scales[:], in_=x_grouped[:])

        codes = {}
        pending = []

        def turn(i, c, engine):
            words = rows[i][:, c, :].bitcast(F32)
            grouped = stage.tile([P, PAIR * P * PACK], BF16, align_bytes=64, tag="w", name="w_grouped")
            if engine == "VS":
                for b, e in enumerate("VS"):
                    bank = banks.tile([P, 1, HALVES, P], F32, tag="bank", name="bank")
                    transposes(words, bank, b, 1)
                    copy_out(e, bank, grouped, b, 1)
            else:
                bank = banks.tile([P, PAIR, HALVES, P], F32, tag="bank", name="bank")
                transposes(words, bank, 0, PAIR)
                copy_out(engine, bank, grouped, 0, PAIR)
            pending.append((i, c, grouped))

        def quantise():
            i, c, grouped = pending.pop(0)
            q = keep.tile([P, UNIT_FEATURES], U32, align_bytes=64, name="codes%d_%d" % (i, c))
            s = keep.tile([P, UNIT_FEATURES], U8, align_bytes=64, name="scales%d_%d" % (i, c))
            nc.vector.quantize_mx(out=q[:].bitcast(FP8X4), scales=s[:], in_=grouped[:])
            codes[i, c] = (q, s)

        b1_cols = keep.tile([P, GROUPS * PACK], F32)

        def bias_1():
            b1_bank = banks.tile([P, HALVES, P], F32, tag="bank", name="b1_bank")
            for u in range(HALVES):
                nc.tensor.transpose(b1_bank[:, u, :], b1_rows[:].bitcast(F32)[:, u::HALVES], identity[:])
            for u in range(HALVES):
                nc.vector.tensor_copy(
                    out=b1_cols[:].rearrange("p (g u e) -> p u g e", g=GROUPS, u=HALVES)[:, u],
                    in_=b1_bank[:, u, 0:GROUPS].bitcast(BF16).rearrange("p (g e) -> p g e", e=2),
                )

        def layer_1(g):
            y_bank = y_banks.tile([P, PACK, TOKENS], F32, tag="y_bank", name="y_bank")
            for t in range(PACK):
                q, s = codes[g, t // PAIR]
                block = slice((t % PAIR) * P, (t % PAIR + 1) * P)
                nc.tensor.matmul_mx(
                    out=y_bank[:, t, :],
                    lhsT=q[:, block].bitcast(FP8X4),
                    lhsT_scale=s[:, block],
                    rhs=x_codes[:].bitcast(FP8X4),
                    rhs_scale=x_scales[:],
                    start=True,
                    stop=True,
                )
            own = slice(g * GROUP_TOKENS, (g + 1) * GROUP_TOKENS)
            nc.vector.tensor_tensor(
                out=y_grouped[:, g, own, :],
                in0=y_bank[:, :, own].rearrange("p c t -> p t c"),
                in1=b1_cols[:, g * PACK : (g + 1) * PACK].unsqueeze(1).to_broadcast([P, GROUP_TOKENS, PACK]),
                op=ADD,
            )

        def quantise_y(g):
            nc.vector.quantize_mx(
                out=y_codes[:, g, :].bitcast(FP8X4),
                scales=y_scales[:, g, :],
                in_=y_grouped[:, g].rearrange("p t c -> p (t c)"),
            )

        acc = [sums.tile([P, UNIT_FEATURES], F32, name="acc%d" % c) for c in range(UNITS)]

        def layer_2(g, c):
            q, s = codes[GROUPS + g, c]
            nc.tensor.matmul_mx(
                out=acc[c][:],
                lhsT=y_codes[:, g, :].bitcast(FP8X4),
                lhsT_scale=y_scales[:, g, :],
                rhs=q[:].bitcast(FP8X4),
                rhs_scale=s[:],
                start=(g == 0),
                stop=(g == GROUPS - 1),
            )

        turn(0, 0, "S")
        turn(0, 1, "S")
        quantise()
        bias_1()
        turn(1, 0, "S")
        quantise()
        turn(1, 1, "V")
        quantise()
        turn(2, 0, "S")
        quantise()
        turn(2, 1, "S")
        quantise()
        layer_1(0)
        layer_1(1)
        turn(3, 0, "S")
        quantise()
        quantise_y(0)
        quantise_y(1)
        turn(3, 1, "V")
        quantise()
        turn(4, 0, "S")
        quantise()
        turn(4, 1, "S")
        quantise()
        layer_1(2)
        layer_1(3)
        turn(5, 0, "S")
        quantise()
        quantise_y(2)
        quantise_y(3)
        turn(5, 1, "V")
        quantise()
        turn(6, 0, "S")
        quantise()
        turn(6, 1, "S")
        quantise()
        turn(7, 0, "S")
        quantise()
        turn(7, 1, "VS")
        quantise()
        quantise()
        for c in range(UNITS):
            for g in range(GROUPS - 1):
                layer_2(g, c)
        result = keep.tile([P, FEATURES], F32)
        for c in range(UNITS):
            layer_2(GROUPS - 1, c)
        for c in range(UNITS):
            cols = slice(c * UNIT_FEATURES, (c + 1) * UNIT_FEATURES)
            nc.vector.tensor_tensor(
                out=result[:, cols].rearrange("p (r j) -> p r j", j=PAIR),
                in0=acc[c][:].rearrange("p (j r) -> p r j", j=PAIR),
                in1=b2_rows[:, cols].rearrange("p (r j) -> p r j", j=PAIR),
                op=ADD,
            )
            nc.sync.dma_start(out=out[:, cols], in_=result[:, cols])
